import numpy as np
import ml_dtypes


def mxq(x, axis, fmt="e4m3"):
    dtype, down = {"e4m3": (ml_dtypes.float8_e4m3fn, 7), "e5m2": (ml_dtypes.float8_e5m2, 14)}[fmt]
    v = np.moveaxis(np.asarray(x, np.float32).astype(ml_dtypes.bfloat16).astype(np.float64), axis, -1)
    blocks = v.reshape(v.shape[:-1] + (-1, 32))
    amax = np.abs(blocks).max(-1, keepdims=True)
    byte = np.maximum(np.where(amax > 0, np.frexp(amax)[1] - 1 + 127, 0) - down, 1)
    scale = np.exp2(byte - 127.0)
    codes = (blocks / scale).astype(np.float32).astype(dtype).astype(np.float64)
    return np.moveaxis((codes * scale).reshape(v.shape), -1, axis)


WIDE = False


def mx_kscale(k):
    if not WIDE:
        return np.ones(k)
    levels = np.array([10, -10, 5, -5, 0])
    a = np.random.permutation(np.resize(levels, k // 512 * 4)).reshape(k // 512, 4)
    idx = np.arange(k)
    return np.exp2(a[idx // 512, idx % 128 // 32])


BF16 = ml_dtypes.bfloat16


def bf(x):
    return np.asarray(x, np.float32).astype(BF16)


def f64(x):
    return np.asarray(x).astype(np.float64)


B, N, DIN, DH, DOUT = 256, 4, 512, 512, 512
KH = N * DH
KO = N * DOUT
EPS = 1e-5


def elu(v):
    return np.where(v > 0.0, v, np.expm1(np.minimum(v, 0.0)))


def sigmoid(v):
    return 1.0 / (1.0 + np.exp(-v))


def setup_inputs():
    rn = np.random.standard_normal
    s, t = mx_kscale(KH), mx_kscale(KO)
    return {
        "h": bf(elu(rn((B, KH))) * s),
        "x": bf(rn((B, N, DIN)) + 0.5),
        "cW1": bf(rn((KH, KO)) * 1.2 / np.sqrt(KH) / s[:, None] * t),
        "cb1": bf(rn(KO) * 0.3 * t),
        "cW4": bf(rn((KO, KO)) / np.sqrt(KO) / t[:, None]),
        "cb4": bf(rn(KO) * 0.3),
        "cW5": bf(rn((KO, KO)) / np.sqrt(KO) / t[:, None]),
        "cb5": bf(rn(KO) * 0.3),
        "clng": bf(1.0 + 0.2 * rn(KO)),
        "clnb": bf(0.2 * rn(KO)),
    }


def reference(h, x, cW1, cb1, cW4, cb4, cW5, cb5, clng, clnb):
    flat = f64(x).reshape(B, N * DIN)
    e1 = (mxq(f64(h), 1, "e4m3") @ mxq(f64(cW1), 0, "e4m3")) + f64(cb1)
    e1q = mxq(e1, 1, "e4m3")
    g = sigmoid((e1q @ mxq(f64(cW4), 0, "e4m3")) + f64(cb4)) * ((e1q @ mxq(f64(cW5), 0, "e4m3")) + f64(cb5))
    r = flat + g
    c = (r - r.mean(-1, keepdims=True)) * (1.0 / np.sqrt(r.var(-1, keepdims=True) + EPS)) * f64(clng) + f64(clnb)
    c = c.reshape(B, N, DOUT)
    e = np.exp(c - c.max(1, keepdims=True))
    return e / e.sum(1, keepdims=True)

@@ -1,0 +1,316 @@
+from contextlib import ExitStack
+
+import concourse.mybir as mybir
+from concourse.masks import make_identity
+
+FLOPS = 2 * 256 * 2048 * 2048 * 3
+
+BF16 = mybir.dt.bfloat16
+F32 = mybir.dt.float32
+U32 = mybir.dt.uint32
+U8 = mybir.dt.uint8
+FP8X4 = mybir.dt.float8_e4m3fn_x4
+ALU = mybir.AluOpType
+ACT = mybir.ActivationFunctionType
+AXIS = mybir.AxisListType
+
+P = 128
+PACK = 4
+K_PASS = P * PACK
+BATCH = 256
+BATCH_TILES = BATCH // P
+WIDTH = 2048
+PASSES = WIDTH // K_PASS
+VARIABLES = 4
+FEATURES = WIDTH // VARIABLES
+HALF = WIDTH // 2
+HALVES = 2
+SLICES_PER_HALF = HALF // P
+SLICES_PER_VARIABLE = FEATURES // P
+EPS = 1e-5
+VECTOR_COLS = 448
+
+
+def word_order(dst, src):
+    return (
+        dst.rearrange("p (c i) t -> p c t i", i=4),
+        src.rearrange("p t (c i) -> p c t i", i=4),
+    )
+
+
+def tile_variableselectionnetwork_pa_kernel(
+    tc, h, x, cW1, cb1, cW4, cb4, cW5, cb5, clng, clnb, out
+):
+    nc = tc.nc
+    x_rows = x.rearrange("b v f -> b (v f)")
+    out_rows = out.rearrange("b v f -> b (v f)")
+
+    with ExitStack() as whole:
+        keep = whole.enter_context(tc.tile_pool(name="keep", bufs=1))
+        sums = whole.enter_context(tc.psum_pool(name="sums", bufs=4))
+        flips_bf = whole.enter_context(tc.psum_pool(name="flips_bf", bufs=2))
+        flips_f32 = whole.enter_context(tc.psum_pool(name="flips_f32", bufs=2))
+
+        ident_bf = keep.tile([P, P], BF16)
+        make_identity(nc, ident_bf[:])
+        ident_f32 = keep.tile([P, P], F32)
+        make_identity(nc, ident_f32[:])
+
+        h_codes = keep.tile([P, PASSES, BATCH], U32, align_bytes=64)
+        h_scales = keep.tile([P, PASSES, BATCH], U8, align_bytes=64)
+        e1_codes = keep.tile([P, PASSES, BATCH], U32, align_bytes=64)
+        e1_scales = keep.tile([P, PASSES, BATCH], U8, align_bytes=64)
+        bias_cols = keep.tile([P, P], F32)
+        x_sb = [keep.tile([P, WIDTH], BF16, name="x_sb%d" % bt) for bt in range(BATCH_TILES)]
+        gain_rows = keep.tile([P, WIDTH], BF16)
+        shift_rows = keep.tile([P, WIDTH], BF16)
+        r = [keep.tile([P, WIDTH], F32, name="r%d" % bt) for bt in range(BATCH_TILES)]
+        r_sums = [keep.tile([P, VARIABLES], F32, name="r_sums%d" % bt) for bt in range(BATCH_TILES)]
+
+        with ExitStack() as stream:
+            raw_pool = stream.enter_context(tc.tile_pool(name="raw", bufs=5))
+            grouped_pool = stream.enter_context(tc.tile_pool(name="grouped", bufs=3))
+            codes_pool = stream.enter_context(tc.tile_pool(name="codes", bufs=3))
+            e1_pool = stream.enter_context(tc.tile_pool(name="e1", bufs=1))
+            gate_pool = stream.enter_context(tc.tile_pool(name="gate", bufs=2))
+            gated_pool = stream.enter_context(tc.tile_pool(name="gated", bufs=4))
+
+            with tc.tile_pool(name="head", bufs=1) as head:
+                h_rows = []
+                for bt in range(BATCH_TILES):
+                    rows = head.tile([P, WIDTH], BF16, name="h_rows%d" % bt)
+                    nc.sync.dma_start(out=rows[:], in_=h[bt * P : (bt + 1) * P, :])
+                    h_rows.append(rows)
+
+                bias_rows = head.tile([P, P], BF16)
+                nc.vector.memset(bias_rows[:], 0.0)
+                slices = WIDTH // P
+                for i, vec in enumerate((cb1, cb4, cb5)):
+                    nc.scalar.dma_start(
+                        out=bias_rows[i * slices : (i + 1) * slices, :],
+                        in_=vec.rearrange("(s p) -> s p", p=P),
+                    )
+                bias_flip = flips_bf.tile([P, P], BF16, tag="flip_bf")
+                nc.tensor.transpose(out=bias_flip[:], in_=bias_rows[:], identity=ident_bf[:])
+                nc.vector.tensor_copy(out=bias_cols[:], in_=bias_flip[:])
+
+                h_grouped = head.tile([P, PASSES, BATCH, PACK], BF16, align_bytes=64)
+                for g in range(PASSES):
+                    h_flip = flips_bf.tile([P, PACK, BATCH], BF16, tag="flip_bf")
+                    for t in range(PACK):
+                        k0 = g * K_PASS + t * P
+                        for bt in range(BATCH_TILES):
+                            nc.tensor.transpose(
+                                out=h_flip[:, t, bt * P : (bt + 1) * P],
+                                in_=h_rows[bt][:, k0 : k0 + P],
+                                identity=ident_bf[:],
+                            )
+                    copy_out = nc.vector.tensor_copy if g % 2 == 0 else nc.scalar.copy
+                    copy_out(out=h_grouped[:, g, :, :], in_=h_flip[:].rearrange("p t b -> p b t"))
+                nc.vector.quantize_mx(
+                    out=h_codes[:].rearrange("p g b -> p (g b)").bitcast(FP8X4),
+                    scales=h_scales[:].rearrange("p g b -> p (g b)"),
+                    in_=h_grouped[:].rearrange("p g b t -> p (g b t)"),
+                )
+
+            def quantise_half(w, half):
+                cols = slice(half * HALF, (half + 1) * HALF)
+                codes = codes_pool.tile([P, PASSES, HALF], U32, align_bytes=64)
+                scales = codes_pool.tile([P, PASSES, HALF], U8, align_bytes=64)
+                w_passes = w.rearrange("(g t p) n -> g p t n", t=PACK, p=P)
+                for g in range(PASSES):
+                    raw = raw_pool.tile([P, PACK, HALF], BF16)
+                    nc.sync.dma_start(out=raw[:], in_=w_passes[g][:, :, cols])
+                    grouped = grouped_pool.tile([P, HALF, PACK], BF16, align_bytes=64)
+                    dst, src = word_order(grouped[:, :VECTOR_COLS, :], raw[:, :, :VECTOR_COLS])
+                    nc.vector.tensor_copy(out=dst, in_=src)
+                    dst, src = word_order(grouped[:, VECTOR_COLS:, :], raw[:, :, VECTOR_COLS:])
+                    nc.scalar.copy(out=dst, in_=src)
+                    nc.vector.quantize_mx(
+                        out=codes[:, g, :].bitcast(FP8X4),
+                        scales=scales[:, g, :],
+                        in_=grouped[:].rearrange("p c t -> p (c t)"),
+                    )
+                return codes, scales
+
+            def product_slice(codes, scales, j, act_codes, act_scales):
+                acc = sums.tile([P, BATCH], F32)
+                feats = slice(j * P, (j + 1) * P)
+                for g in range(PASSES):
+                    nc.tensor.matmul_mx(
+                        out=acc[:],
+                        lhsT=codes[:, g, feats].bitcast(FP8X4),
+                        lhsT_scale=scales[:, g, feats],
+                        rhs=act_codes[:, g, :].bitcast(FP8X4),
+                        rhs_scale=act_scales[:, g, :],
+                        start=(g == 0),
+                        stop=(g == PASSES - 1),
+                    )
+                return acc
+
+            e1_bf = e1_pool.tile([P, PASSES, PACK, BATCH], BF16)
+            e1_grouped = e1_pool.tile([P, PASSES, BATCH, PACK], BF16, align_bytes=64)
+            for half in range(HALVES):
+                codes, scales = quantise_half(cW1, half)
+                for j in range(SLICES_PER_HALF):
+                    s = half * SLICES_PER_HALF + j
+                    g2, t2 = divmod(s, PACK)
+                    acc = product_slice(codes, scales, j, h_codes, h_scales)
+                    nc.scalar.activation(
+                        out=e1_bf[:, g2, t2, :],
+                        in_=acc[:],
+                        func=ACT.Identity,
+                        bias=bias_cols[:, s : s + 1],
+                        scale=1.0,
+                    )
+                    if t2 == PACK - 1:
+                        dst, src = word_order(e1_grouped[:, g2, :, :], e1_bf[:, g2, :, :])
+                        nc.vector.tensor_copy(out=dst, in_=src)
+                        nc.vector.quantize_mx(
+                            out=e1_codes[:, g2, :].bitcast(FP8X4),
+                            scales=e1_scales[:, g2, :],
+                            in_=e1_grouped[:, g2, :, :].rearrange("p b t -> p (b t)"),
+                        )
+
+            for bt in range(BATCH_TILES):
+                nc.sync.dma_start(out=x_sb[bt][:], in_=x_rows[bt * P : (bt + 1) * P, :])
+
+            slices = WIDTH // P
+            for half in range(HALVES):
+                codes, scales = quantise_half(cW4, half)
+                gate = gate_pool.tile([P, SLICES_PER_HALF, BATCH], F32)
+                for j in range(SLICES_PER_HALF):
+                    s = half * SLICES_PER_HALF + j
+                    acc = product_slice(codes, scales, j, e1_codes, e1_scales)
+                    nc.scalar.activation(
+                        out=gate[:, j, :],
+                        in_=acc[:],
+                        func=ACT.Sigmoid,
+                        bias=bias_cols[:, slices + s : slices + s + 1],
+                        scale=1.0,
+                    )
+
+                if half == 0:
+                    nc.sync.dma_start(out=gain_rows[:], in_=clng.partition_broadcast(P))
+                    nc.sync.dma_start(out=shift_rows[:], in_=clnb.partition_broadcast(P))
+
+                codes, scales = quantise_half(cW5, half)
+                for v_local in range(SLICES_PER_HALF // SLICES_PER_VARIABLE):
+                    v = half * (VARIABLES // HALVES) + v_local
+                    gated = []
+                    for i in range(SLICES_PER_VARIABLE):
+                        j = v_local * SLICES_PER_VARIABLE + i
+                        s = half * SLICES_PER_HALF + j
+                        acc = product_slice(codes, scales, j, e1_codes, e1_scales)
+                        g_slice = gated_pool.tile([P, BATCH], F32)
+                        nc.vector.scalar_tensor_tensor(
+                            out=g_slice[:],
+                            in0=acc[:],
+                            scalar=bias_cols[:, 2 * slices + s : 2 * slices + s + 1],
+                            in1=gate[:, j, :],
+                            op0=ALU.add,
+                            op1=ALU.mult,
+                        )
+                        gated.append(g_slice)
+                    v_cols = slice(v * FEATURES, (v + 1) * FEATURES)
+                    for bt in range(BATCH_TILES):
+                        g_rows = flips_f32.tile([P, FEATURES], F32)
+                        for i in range(SLICES_PER_VARIABLE):
+                            nc.tensor.transpose(
+                                out=g_rows[:, i * P : (i + 1) * P],
+                                in_=gated[i][:, bt * P : (bt + 1) * P],
+                                identity=ident_f32[:],
+                            )
+                        nc.vector.scalar_tensor_tensor(
+                            out=r[bt][:, v_cols],
+                            in0=g_rows[:],
+                            scalar=1.0,
+                            in1=x_sb[bt][:, v_cols],
+                            op0=ALU.mult,
+                            op1=ALU.add,
+                            accum_out=r_sums[bt][:, v : v + 1],
+                        )
+
+        with tc.tile_pool(name="tail", bufs=2) as tail:
+            minus_half = tail.tile([P, 1], F32, bufs=1)
+            nc.vector.memset(minus_half[:], -0.5)
+
+            centred = []
+            rstd = []
+            for bt in range(BATCH_TILES):
+                total = tail.tile([P, 1], F32)
+                nc.vector.tensor_reduce(out=total[:], in_=r_sums[bt][:], axis=AXIS.X, op=ALU.add)
+                minus_mean = tail.tile([P, 1], F32)
+                nc.vector.tensor_scalar_mul(out=minus_mean[:], in0=total[:], scalar1=-1.0 / WIDTH)
+
+                squares = tail.tile([P, WIDTH], BF16, bufs=1)
+                square_sum = tail.tile([P, 1], F32)
+                nc.scalar.activation(
+                    out=squares[:],
+                    in_=r[bt][:],
+                    func=ACT.Square,
+                    bias=minus_mean[:, 0:1],
+                    scale=1.0,
+                    accum_out=square_sum[:],
+                )
+                var_eps = tail.tile([P, 1], F32)
+                nc.vector.tensor_scalar(
+                    out=var_eps[:],
+                    in0=square_sum[:],
+                    scalar1=1.0 / WIDTH,
+                    scalar2=EPS,
+                    op0=ALU.mult,
+                    op1=ALU.add,
+                )
+                inv_std = tail.tile([P, 1], F32)
+                nc.gpsimd.tensor_tensor(out=inv_std[:], in0=var_eps[:], in1=minus_half[:], op=ALU.pow)
+                rstd.append(inv_std)
+
+                c = tail.tile([P, WIDTH], F32)
+                nc.vector.scalar_tensor_tensor(
+                    out=c[:],
+                    in0=r[bt][:],
+                    scalar=minus_mean[:, 0:1],
+                    in1=gain_rows[:],
+                    op0=ALU.add,
+                    op1=ALU.mult,
+                )
+                centred.append(c)
+
+            exps = []
+            for bt in range(BATCH_TILES):
+                c = centred[bt]
+                nc.vector.scalar_tensor_tensor(
+                    out=c[:],
+                    in0=c[:],
+                    scalar=rstd[bt][:, 0:1],
+                    in1=shift_rows[:],
+                    op0=ALU.mult,
+                    op1=ALU.add,
+                )
+                top2 = tail.tile([P, 2 * FEATURES], F32, tag="pair")
+                nc.vector.tensor_max(out=top2[:], in0=c[:, : 2 * FEATURES], in1=c[:, 2 * FEATURES :])
+                top = tail.tile([P, FEATURES], F32)
+                nc.vector.tensor_max(out=top[:], in0=top2[:, :FEATURES], in1=top2[:, FEATURES:])
+                c_by_variable = c[:].rearrange("p (v f) -> p v f", v=VARIABLES)
+                nc.vector.tensor_sub(
+                    out=c_by_variable,
+                    in0=c_by_variable,
+                    in1=top[:].unsqueeze(1).to_broadcast([P, VARIABLES, FEATURES]),
+                )
+                e = r[bt]
+                nc.scalar.activation(out=e[:], in_=c[:], func=ACT.Exp)
+                exps.append(e)
+
+            for bt in range(BATCH_TILES):
+                e = exps[bt]
+                sum2 = tail.tile([P, 2 * FEATURES], F32, tag="pair")
+                nc.vector.tensor_add(out=sum2[:], in0=e[:, : 2 * FEATURES], in1=e[:, 2 * FEATURES :])
+                denom = tail.tile([P, FEATURES], F32)
+                nc.vector.tensor_add(out=denom[:], in0=sum2[:, :FEATURES], in1=sum2[:, FEATURES:])
+                inv_denom = tail.tile([P, FEATURES], F32)
+                nc.vector.reciprocal(out=inv_denom[:], in_=denom[:])
+                for v in range(VARIABLES):
+                    v_cols = slice(v * FEATURES, (v + 1) * FEATURES)
+                    nc.vector.tensor_mul(out=e[:, v_cols], in0=e[:, v_cols], in1=inv_denom[:])
+                    nc.sync.dma_start(out=out_rows[bt * P : (bt + 1) * P, v_cols], in_=e[:, v_cols])

@@ -27,8 +27,15 @@ HALF = WIDTH // 2
 HALVES = 2
 SLICES_PER_HALF = HALF // P
 SLICES_PER_VARIABLE = FEATURES // P
+SLICES = WIDTH // P
+GROUPS = SLICES_PER_VARIABLE
 EPS = 1e-5
-VECTOR_COLS = 448
+CB1 = 0
+CB4 = 1
+CB5 = 2
+GAIN = 3
+SHIFT = 4
+VECTOR_COLS = 544
 
 
 def word_order(dst, src):
@@ -43,14 +50,8 @@ def tile_variableselectionnetwork_pa_kernel(
 ):
     nc = tc.nc
     x_rows = x.rearrange("b v f -> b (v f)")
-    out_rows = out.rearrange("b v f -> b (v f)")
 
-    with ExitStack() as whole:
-        keep = whole.enter_context(tc.tile_pool(name="keep", bufs=1))
-        sums = whole.enter_context(tc.psum_pool(name="sums", bufs=4))
-        flips_bf = whole.enter_context(tc.psum_pool(name="flips_bf", bufs=2))
-        flips_f32 = whole.enter_context(tc.psum_pool(name="flips_f32", bufs=2))
-
+    with tc.tile_pool(name="keep", bufs=1) as keep:
         ident_bf = keep.tile([P, P], BF16)
         make_identity(nc, ident_bf[:])
         ident_f32 = keep.tile([P, P], F32)
@@ -60,12 +61,16 @@ def tile_variableselectionnetwork_pa_kernel(
         h_scales = keep.tile([P, PASSES, BATCH], U8, align_bytes=64)
         e1_codes = keep.tile([P, PASSES, BATCH], U32, align_bytes=64)
         e1_scales = keep.tile([P, PASSES, BATCH], U8, align_bytes=64)
-        bias_cols = keep.tile([P, P], F32)
         x_sb = [keep.tile([P, WIDTH], BF16, name="x_sb%d" % bt) for bt in range(BATCH_TILES)]
-        gain_rows = keep.tile([P, WIDTH], BF16)
-        shift_rows = keep.tile([P, WIDTH], BF16)
         r = [keep.tile([P, WIDTH], F32, name="r%d" % bt) for bt in range(BATCH_TILES)]
-        r_sums = [keep.tile([P, VARIABLES], F32, name="r_sums%d" % bt) for bt in range(BATCH_TILES)]
+        r_sums = keep.tile([P, BATCH_TILES, VARIABLES], F32)
+        minus_shift = keep.tile([P, BATCH_TILES], F32)
+        square_sums = keep.tile([P, BATCH_TILES, VARIABLES], F32)
+
+        vector_cols = keep.tile([P, P], F32)
+
+        def vector_col(i, s):
+            return vector_cols[:, i * SLICES + s : i * SLICES + s + 1]
 
         with ExitStack() as stream:
             raw_pool = stream.enter_context(tc.tile_pool(name="raw", bufs=5))
@@ -74,6 +79,9 @@ def tile_variableselectionnetwork_pa_kernel(
             e1_pool = stream.enter_context(tc.tile_pool(name="e1", bufs=1))
             gate_pool = stream.enter_context(tc.tile_pool(name="gate", bufs=2))
             gated_pool = stream.enter_context(tc.tile_pool(name="gated", bufs=4))
+            sums = stream.enter_context(tc.psum_pool(name="sums", bufs=4))
+            flips_bf = stream.enter_context(tc.psum_pool(name="flips_bf", bufs=2))
+            flips_f32 = stream.enter_context(tc.psum_pool(name="flips_f32", bufs=2))
 
             with tc.tile_pool(name="head", bufs=1) as head:
                 h_rows = []
@@ -82,17 +90,13 @@ def tile_variableselectionnetwork_pa_kernel(
                     nc.sync.dma_start(out=rows[:], in_=h[bt * P : (bt + 1) * P, :])
                     h_rows.append(rows)
 
-                bias_rows = head.tile([P, P], BF16)
-                nc.vector.memset(bias_rows[:], 0.0)
-                slices = WIDTH // P
-                for i, vec in enumerate((cb1, cb4, cb5)):
+                vector_rows = head.tile([P, P], BF16)
+                nc.vector.memset(vector_rows[:], 0.0)
+                for i, vec in enumerate((cb1, cb4, cb5, clng, clnb)):
                     nc.scalar.dma_start(
-                        out=bias_rows[i * slices : (i + 1) * slices, :],
+                        out=vector_rows[i * SLICES : (i + 1) * SLICES, :],
                         in_=vec.rearrange("(s p) -> s p", p=P),
                     )
-                bias_flip = flips_bf.tile([P, P], BF16, tag="flip_bf")
-                nc.tensor.transpose(out=bias_flip[:], in_=bias_rows[:], identity=ident_bf[:])
-                nc.vector.tensor_copy(out=bias_cols[:], in_=bias_flip[:])
 
                 h_grouped = head.tile([P, PASSES, BATCH, PACK], BF16, align_bytes=64)
                 for g in range(PASSES):
@@ -112,6 +116,10 @@ def tile_variableselectionnetwork_pa_kernel(
                     scales=h_scales[:].rearrange("p g b -> p (g b)"),
                     in_=h_grouped[:].rearrange("p g b t -> p (g b t)"),
                 )
+
+                vector_flip = flips_bf.tile([P, P], BF16, tag="flip_bf")
+                nc.tensor.transpose(out=vector_flip[:], in_=vector_rows[:], identity=ident_bf[:])
+                nc.vector.tensor_copy(out=vector_cols[:], in_=vector_flip[:])
 
             def quantise_half(w, half):
                 cols = slice(half * HALF, (half + 1) * HALF)
@@ -160,7 +168,7 @@ def tile_variableselectionnetwork_pa_kernel(
                         out=e1_bf[:, g2, t2, :],
                         in_=acc[:],
                         func=ACT.Identity,
-                        bias=bias_cols[:, s : s + 1],
+                        bias=vector_col(CB1, s),
                         scale=1.0,
                     )
                     if t2 == PACK - 1:
@@ -175,7 +183,6 @@ def tile_variableselectionnetwork_pa_kernel(
             for bt in range(BATCH_TILES):
                 nc.sync.dma_start(out=x_sb[bt][:], in_=x_rows[bt * P : (bt + 1) * P, :])
 
-            slices = WIDTH // P
             for half in range(HALVES):
                 codes, scales = quantise_half(cW4, half)
                 gate = gate_pool.tile([P, SLICES_PER_HALF, BATCH], F32)
@@ -186,13 +193,12 @@ def tile_variableselectionnetwork_pa_kernel(
                         out=gate[:, j, :],
                         in_=acc[:],
                         func=ACT.Sigmoid,
-                        bias=bias_cols[:, slices + s : slices + s + 1],
+                        bias=vector_col(CB4, s),
                         scale=1.0,
                     )
-
-                if half == 0:
-                    nc.sync.dma_start(out=gain_rows[:], in_=clng.partition_broadcast(P))
-                    nc.sync.dma_start(out=shift_rows[:], in_=clnb.partition_broadcast(P))
+                if half == HALVES - 1:
+                    warm = gate_pool.tile([P, 1], F32)
+                    nc.scalar.activation(out=warm[:], in_=ident_f32[:, 0:1], func=ACT.Exp)
 
                 codes, scales = quantise_half(cW5, half)
                 for v_local in range(SLICES_PER_HALF // SLICES_PER_VARIABLE):
@@ -206,7 +212,7 @@ def tile_variableselectionnetwork_pa_kernel(
                         nc.vector.scalar_tensor_tensor(
                             out=g_slice[:],
                             in0=acc[:],
-                            scalar=bias_cols[:, 2 * slices + s : 2 * slices + s + 1],
+                            scalar=vector_col(CB5, s),
                             in1=gate[:, j, :],
                             op0=ALU.add,
                             op1=ALU.mult,
@@ -228,89 +234,145 @@ def tile_variableselectionnetwork_pa_kernel(
                             in1=x_sb[bt][:, v_cols],
                             op0=ALU.mult,
                             op1=ALU.add,
-                            accum_out=r_sums[bt][:, v : v + 1],
+                            accum_out=r_sums[:, bt, v : v + 1],
+                        )
+                        if v == 0:
+                            nc.vector.tensor_scalar_mul(
+                                out=minus_shift[:, bt : bt + 1],
+                                in0=r_sums[:, bt, 0:1],
+                                scalar1=-1.0 / FEATURES,
+                            )
+                        squares = gated_pool.tile([P, FEATURES], BF16)
+                        nc.scalar.activation(
+                            out=squares[:],
+                            in_=r[bt][:, v_cols],
+                            func=ACT.Square,
+                            bias=minus_shift[:, bt : bt + 1],
+                            scale=1.0,
+                            accum_out=square_sums[:, bt, v : v + 1],
                         )
 
-        with tc.tile_pool(name="tail", bufs=2) as tail:
-            minus_half = tail.tile([P, 1], F32, bufs=1)
+        with ExitStack() as finish:
+            small = finish.enter_context(tc.tile_pool(name="small", bufs=1))
+            work = finish.enter_context(tc.tile_pool(name="work", bufs=2))
+            per_group = finish.enter_context(tc.tile_pool(name="per_group", bufs=GROUPS))
+            z_flips = finish.enter_context(tc.psum_pool(name="z_flips", bufs=2))
+            e_flips = finish.enter_context(tc.psum_pool(name="e_flips", bufs=4))
+            inv_flips = finish.enter_context(tc.psum_pool(name="inv_flips", bufs=2))
+
+            shape = [P, BATCH_TILES]
+            total = small.tile(shape, F32)
+            nc.vector.tensor_reduce(out=total[:], in_=r_sums[:], axis=AXIS.X, op=ALU.add)
+            square_total = small.tile(shape, F32)
+            nc.vector.tensor_reduce(out=square_total[:], in_=square_sums[:], axis=AXIS.X, op=ALU.add)
+            minus_mean = small.tile(shape, F32)
+            nc.vector.tensor_scalar_mul(out=minus_mean[:], in0=total[:], scalar1=-1.0 / WIDTH)
+            offset = small.tile(shape, F32)
+            nc.vector.tensor_sub(out=offset[:], in0=minus_mean[:], in1=minus_shift[:])
+            minus_offset2 = small.tile(shape, F32)
+            nc.vector.scalar_tensor_tensor(
+                out=minus_offset2[:], in0=offset[:], scalar=-1.0, in1=offset[:], op0=ALU.mult, op1=ALU.mult
+            )
+            var = small.tile(shape, F32)
+            nc.vector.scalar_tensor_tensor(
+                out=var[:],
+                in0=square_total[:],
+                scalar=1.0 / WIDTH,
+                in1=minus_offset2[:],
+                op0=ALU.mult,
+                op1=ALU.add,
+            )
+            var_eps = small.tile(shape, F32)
+            nc.vector.tensor_scalar(
+                out=var_eps[:], in0=var[:], scalar1=0.0, scalar2=EPS, op0=ALU.max, op1=ALU.add
+            )
+            minus_half = small.tile(shape, F32)
             nc.vector.memset(minus_half[:], -0.5)
-
-            centred = []
-            rstd = []
-            for bt in range(BATCH_TILES):
-                total = tail.tile([P, 1], F32)
-                nc.vector.tensor_reduce(out=total[:], in_=r_sums[bt][:], axis=AXIS.X, op=ALU.add)
-                minus_mean = tail.tile([P, 1], F32)
-                nc.vector.tensor_scalar_mul(out=minus_mean[:], in0=total[:], scalar1=-1.0 / WIDTH)
-
-                squares = tail.tile([P, WIDTH], BF16, bufs=1)
-                square_sum = tail.tile([P, 1], F32)
-                nc.scalar.activation(
-                    out=squares[:],
-                    in_=r[bt][:],
-                    func=ACT.Square,
-                    bias=minus_mean[:, 0:1],
-                    scale=1.0,
-                    accum_out=square_sum[:],
-                )
-                var_eps = tail.tile([P, 1], F32)
-                nc.vector.tensor_scalar(
-                    out=var_eps[:],
-                    in0=square_sum[:],
-                    scalar1=1.0 / WIDTH,
-                    scalar2=EPS,
-                    op0=ALU.mult,
-                    op1=ALU.add,
-                )
-                inv_std = tail.tile([P, 1], F32)
-                nc.gpsimd.tensor_tensor(out=inv_std[:], in0=var_eps[:], in1=minus_half[:], op=ALU.pow)
-                rstd.append(inv_std)
-
-                c = tail.tile([P, WIDTH], F32)
-                nc.vector.scalar_tensor_tensor(
-                    out=c[:],
-                    in0=r[bt][:],
-                    scalar=minus_mean[:, 0:1],
-                    in1=gain_rows[:],
-                    op0=ALU.add,
-                    op1=ALU.mult,
-                )
-                centred.append(c)
+            rstd = small.tile(shape, F32)
+            nc.gpsimd.tensor_tensor(out=rstd[:], in0=var_eps[:], in1=minus_half[:], op=ALU.pow)
 
             exps = []
-            for bt in range(BATCH_TILES):
-                c = centred[bt]
-                nc.vector.scalar_tensor_tensor(
-                    out=c[:],
-                    in0=c[:],
-                    scalar=rstd[bt][:, 0:1],
-                    in1=shift_rows[:],
-                    op0=ALU.mult,
-                    op1=ALU.add,
-                )
-                top2 = tail.tile([P, 2 * FEATURES], F32, tag="pair")
-                nc.vector.tensor_max(out=top2[:], in0=c[:, : 2 * FEATURES], in1=c[:, 2 * FEATURES :])
-                top = tail.tile([P, FEATURES], F32)
-                nc.vector.tensor_max(out=top[:], in0=top2[:, :FEATURES], in1=top2[:, FEATURES:])
-                c_by_variable = c[:].rearrange("p (v f) -> p v f", v=VARIABLES)
-                nc.vector.tensor_sub(
-                    out=c_by_variable,
-                    in0=c_by_variable,
-                    in1=top[:].unsqueeze(1).to_broadcast([P, VARIABLES, FEATURES]),
-                )
-                e = r[bt]
-                nc.scalar.activation(out=e[:], in_=c[:], func=ACT.Exp)
-                exps.append(e)
-
-            for bt in range(BATCH_TILES):
-                e = exps[bt]
-                sum2 = tail.tile([P, 2 * FEATURES], F32, tag="pair")
-                nc.vector.tensor_add(out=sum2[:], in0=e[:, : 2 * FEATURES], in1=e[:, 2 * FEATURES :])
-                denom = tail.tile([P, FEATURES], F32)
-                nc.vector.tensor_add(out=denom[:], in0=sum2[:, :FEATURES], in1=sum2[:, FEATURES:])
-                inv_denom = tail.tile([P, FEATURES], F32)
-                nc.vector.reciprocal(out=inv_denom[:], in_=denom[:])
+            for j in range(GROUPS):
+                f_cols = slice(j * P, (j + 1) * P)
+                z_cols = [
+                    z_flips.tile([P, 2, BATCH], F32, name="z_cols%d" % pair, tag="z_cols")
+                    for pair in range(VARIABLES // 2)
+                ]
+                for bt in range(BATCH_TILES):
+                    z = work.tile([P, VARIABLES, P], F32, bufs=4)
+                    nc.vector.tensor_scalar(
+                        out=z[:],
+                        in0=r[bt][:].rearrange("p (v f) -> p v f", v=VARIABLES)[:, :, f_cols],
+                        scalar1=minus_mean[:, bt : bt + 1],
+                        scalar2=rstd[:, bt : bt + 1],
+                        op0=ALU.add,
+                        op1=ALU.mult,
+                    )
+                    for v in range(VARIABLES):
+                        nc.tensor.transpose(
+                            out=z_cols[v // 2][:, v % 2, bt * P : (bt + 1) * P],
+                            in_=z[:, v, :],
+                            identity=ident_f32[:],
+                        )
+                c = per_group.tile([P, VARIABLES, BATCH], F32)
                 for v in range(VARIABLES):
-                    v_cols = slice(v * FEATURES, (v + 1) * FEATURES)
-                    nc.vector.tensor_mul(out=e[:, v_cols], in0=e[:, v_cols], in1=inv_denom[:])
-                    nc.sync.dma_start(out=out_rows[bt * P : (bt + 1) * P, v_cols], in_=e[:, v_cols])
+                    s = v * SLICES_PER_VARIABLE + j
+                    nc.scalar.activation(
+                        out=c[:, v, :],
+                        in_=z_cols[v // 2][:, v % 2, :],
+                        func=ACT.Identity,
+                        scale=vector_col(GAIN, s),
+                        bias=vector_col(SHIFT, s),
+                    )
+                top2 = work.tile([P, 2, BATCH], F32, tag="pair")
+                nc.vector.tensor_max(out=top2[:], in0=c[:, 0:2, :], in1=c[:, 2:4, :])
+                top = work.tile([P, BATCH], F32)
+                nc.vector.tensor_max(out=top[:], in0=top2[:, 0, :], in1=top2[:, 1, :])
+                nc.vector.tensor_sub(
+                    out=c[:], in0=c[:], in1=top[:].unsqueeze(1).to_broadcast([P, VARIABLES, BATCH])
+                )
+                nc.scalar.activation(out=c[:], in_=c[:], func=ACT.Exp)
+                exps.append(c)
+
+            inverses = []
+            for j in range(GROUPS):
+                e = exps[j]
+                sum2 = work.tile([P, 2, BATCH], F32, tag="pair")
+                nc.vector.tensor_add(out=sum2[:], in0=e[:, 0:2, :], in1=e[:, 2:4, :])
+                denom = per_group.tile([P, BATCH], F32)
+                nc.vector.tensor_add(out=denom[:], in0=sum2[:, 0, :], in1=sum2[:, 1, :])
+                inverses.append(denom)
+            for j in range(GROUPS):
+                inv = inverses[j]
+                nc.scalar.activation(out=inv[:], in_=inv[:], func=ACT.Abs_reciprocal_sqrt)
+                nc.scalar.activation(out=inv[:], in_=inv[:], func=ACT.Square)
+
+            for j in range(GROUPS):
+                f_cols = slice(j * P, (j + 1) * P)
+                e_rows = []
+                for bt in range(BATCH_TILES):
+                    rows = e_flips.tile([P, VARIABLES, P], F32, name="e_rows%d" % bt, tag="e_rows")
+                    for v in range(VARIABLES):
+                        nc.tensor.transpose(
+                            out=rows[:, v, :],
+                            in_=exps[j][:, v, bt * P : (bt + 1) * P],
+                            identity=ident_f32[:],
+                        )
+                    e_rows.append(rows)
+                inv_flip = inv_flips.tile([P, BATCH_TILES, P], F32)
+                for bt in range(BATCH_TILES):
+                    nc.tensor.transpose(
+                        out=inv_flip[:, bt, :],
+                        in_=inverses[j][:, bt * P : (bt + 1) * P],
+                        identity=ident_f32[:],
+                    )
+                inv_rows = work.tile([P, BATCH_TILES, P], F32)
+                nc.scalar.copy(out=inv_rows[:], in_=inv_flip[:])
+                for bt in range(BATCH_TILES):
+                    result = work.tile([P, VARIABLES, P], F32, bufs=4)
+                    nc.vector.tensor_mul(
+                        out=result[:],
+                        in0=e_rows[bt][:],
+                        in1=inv_rows[:, bt, :].unsqueeze(1).to_broadcast([P, VARIABLES, P]),
+                    )
+                    nc.sync.dma_start(out=out[bt * P : (bt + 1) * P, :, f_cols], in_=result[:])

@@ -24,8 +24,6 @@ PASSES = WIDTH // K_PASS
 VARIABLES = 4
 FEATURES = WIDTH // VARIABLES
 HALF = WIDTH // 2
-HALVES = 2
-SLICES_PER_HALF = HALF // P
 SLICES_PER_VARIABLE = FEATURES // P
 SLICES = WIDTH // P
 GROUPS = SLICES_PER_VARIABLE
@@ -35,7 +33,8 @@ CB4 = 1
 CB5 = 2
 GAIN = 3
 SHIFT = 4
-VECTOR_COLS = 544
+FIRST_LAYER_RANGES = ((0, HALF), (HALF, HALF))
+SECOND_LAYER_RANGES = ((0, HALF), (HALF, FEATURES), (HALF + FEATURES, FEATURES))
 
 
 def word_order(dst, src):
@@ -121,18 +120,18 @@ def tile_variableselectionnetwork_pa_kernel(
                 nc.tensor.transpose(out=vector_flip[:], in_=vector_rows[:], identity=ident_bf[:])
                 nc.vector.tensor_copy(out=vector_cols[:], in_=vector_flip[:])
 
-            def quantise_half(w, half):
-                cols = slice(half * HALF, (half + 1) * HALF)
-                codes = codes_pool.tile([P, PASSES, HALF], U32, align_bytes=64)
-                scales = codes_pool.tile([P, PASSES, HALF], U8, align_bytes=64)
+            def quantise_columns(w, first, width):
+                codes = codes_pool.tile([P, PASSES, width], U32, align_bytes=64, tag="codes")
+                scales = codes_pool.tile([P, PASSES, width], U8, align_bytes=64, tag="scales")
                 w_passes = w.rearrange("(g t p) n -> g p t n", t=PACK, p=P)
+                split = width // 2
                 for g in range(PASSES):
-                    raw = raw_pool.tile([P, PACK, HALF], BF16)
-                    nc.sync.dma_start(out=raw[:], in_=w_passes[g][:, :, cols])
-                    grouped = grouped_pool.tile([P, HALF, PACK], BF16, align_bytes=64)
-                    dst, src = word_order(grouped[:, :VECTOR_COLS, :], raw[:, :, :VECTOR_COLS])
+                    raw = raw_pool.tile([P, PACK, width], BF16, tag="raw")
+                    nc.sync.dma_start(out=raw[:], in_=w_passes[g][:, :, first : first + width])
+                    grouped = grouped_pool.tile([P, width, PACK], BF16, align_bytes=64, tag="grouped")
+                    dst, src = word_order(grouped[:, :split, :], raw[:, :, :split])
                     nc.vector.tensor_copy(out=dst, in_=src)
-                    dst, src = word_order(grouped[:, VECTOR_COLS:, :], raw[:, :, VECTOR_COLS:])
+                    dst, src = word_order(grouped[:, split:, :], raw[:, :, split:])
                     nc.scalar.copy(out=dst, in_=src)
                     nc.vector.quantize_mx(
                         out=codes[:, g, :].bitcast(FP8X4),
@@ -158,10 +157,10 @@ def tile_variableselectionnetwork_pa_kernel(
 
             e1_bf = e1_pool.tile([P, PASSES, PACK, BATCH], BF16)
             e1_grouped = e1_pool.tile([P, PASSES, BATCH, PACK], BF16, align_bytes=64)
-            for half in range(HALVES):
-                codes, scales = quantise_half(cW1, half)
-                for j in range(SLICES_PER_HALF):
-                    s = half * SLICES_PER_HALF + j
+            for first, width in FIRST_LAYER_RANGES:
+                codes, scales = quantise_columns(cW1, first, width)
+                for j in range(width // P):
+                    s = first // P + j
                     g2, t2 = divmod(s, PACK)
                     acc = product_slice(codes, scales, j, h_codes, h_scales)
                     nc.scalar.activation(
@@ -183,11 +182,11 @@ def tile_variableselectionnetwork_pa_kernel(
             for bt in range(BATCH_TILES):
                 nc.sync.dma_start(out=x_sb[bt][:], in_=x_rows[bt * P : (bt + 1) * P, :])
 
-            for half in range(HALVES):
-                codes, scales = quantise_half(cW4, half)
-                gate = gate_pool.tile([P, SLICES_PER_HALF, BATCH], F32)
-                for j in range(SLICES_PER_HALF):
-                    s = half * SLICES_PER_HALF + j
+            for first, width in SECOND_LAYER_RANGES:
+                codes, scales = quantise_columns(cW4, first, width)
+                gate = gate_pool.tile([P, HALF // P, BATCH], F32)
+                for j in range(width // P):
+                    s = first // P + j
                     acc = product_slice(codes, scales, j, e1_codes, e1_scales)
                     nc.scalar.activation(
                         out=gate[:, j, :],
@@ -196,17 +195,19 @@ def tile_variableselectionnetwork_pa_kernel(
                         bias=vector_col(CB4, s),
                         scale=1.0,
                     )
-                if half == HALVES - 1:
+                if first + width == WIDTH:
                     warm = gate_pool.tile([P, 1], F32)
-                    nc.scalar.activation(out=warm[:], in_=ident_f32[:, 0:1], func=ACT.Exp)
+                    nc.scalar.activation(
+                        out=warm[:], in_=ident_f32[:, 0:1], func=ACT.Abs_reciprocal_sqrt, bias=1.0
+                    )
 
-                codes, scales = quantise_half(cW5, half)
-                for v_local in range(SLICES_PER_HALF // SLICES_PER_VARIABLE):
-                    v = half * (VARIABLES // HALVES) + v_local
+                codes, scales = quantise_columns(cW5, first, width)
+                for v_local in range(width // FEATURES):
+                    v = first // FEATURES + v_local
                     gated = []
                     for i in range(SLICES_PER_VARIABLE):
                         j = v_local * SLICES_PER_VARIABLE + i
-                        s = half * SLICES_PER_HALF + j
+                        s = first // P + j
                         acc = product_slice(codes, scales, j, e1_codes, e1_scales)
                         g_slice = gated_pool.tile([P, BATCH], F32)
                         nc.vector.scalar_tensor_tensor(
@@ -253,18 +254,16 @@ def tile_variableselectionnetwork_pa_kernel(
                         )
 
         with ExitStack() as finish:
+            finish.enter_context(tc.manual_schedule())
             small = finish.enter_context(tc.tile_pool(name="small", bufs=1))
-            work = finish.enter_context(tc.tile_pool(name="work", bufs=2))
+            work = finish.enter_context(tc.tile_pool(name="work", bufs=4))
             per_group = finish.enter_context(tc.tile_pool(name="per_group", bufs=GROUPS))
-            z_flips = finish.enter_context(tc.psum_pool(name="z_flips", bufs=2))
-            e_flips = finish.enter_context(tc.psum_pool(name="e_flips", bufs=4))
-            inv_flips = finish.enter_context(tc.psum_pool(name="inv_flips", bufs=2))
+            turns = finish.enter_context(tc.psum_pool(name="turns", bufs=8))
 
             shape = [P, BATCH_TILES]
+            last = VARIABLES - 1
             total = small.tile(shape, F32)
             nc.vector.tensor_reduce(out=total[:], in_=r_sums[:], axis=AXIS.X, op=ALU.add)
-            square_total = small.tile(shape, F32)
-            nc.vector.tensor_reduce(out=square_total[:], in_=square_sums[:], axis=AXIS.X, op=ALU.add)
             minus_mean = small.tile(shape, F32)
             nc.vector.tensor_scalar_mul(out=minus_mean[:], in0=total[:], scalar1=-1.0 / WIDTH)
             offset = small.tile(shape, F32)
@@ -273,36 +272,35 @@ def tile_variableselectionnetwork_pa_kernel(
             nc.vector.scalar_tensor_tensor(
                 out=minus_offset2[:], in0=offset[:], scalar=-1.0, in1=offset[:], op0=ALU.mult, op1=ALU.mult
             )
-            var = small.tile(shape, F32)
-            nc.vector.scalar_tensor_tensor(
-                out=var[:],
-                in0=square_total[:],
-                scalar=1.0 / WIDTH,
-                in1=minus_offset2[:],
-                op0=ALU.mult,
-                op1=ALU.add,
-            )
-            var_eps = small.tile(shape, F32)
+            early = small.tile(shape, F32)
+            nc.vector.tensor_reduce(out=early[:], in_=square_sums[:, :, :last], axis=AXIS.X, op=ALU.add)
+            early_eps = small.tile(shape, F32)
             nc.vector.tensor_scalar(
-                out=var_eps[:], in0=var[:], scalar1=0.0, scalar2=EPS, op0=ALU.max, op1=ALU.add
+                out=early_eps[:], in0=early[:], scalar1=1.0 / WIDTH, scalar2=EPS, op0=ALU.mult, op1=ALU.add
             )
-            minus_half = small.tile(shape, F32)
-            nc.vector.memset(minus_half[:], -0.5)
+            root_bias = small.tile(shape, F32)
+            nc.vector.tensor_add(out=root_bias[:], in0=early_eps[:], in1=minus_offset2[:])
             rstd = small.tile(shape, F32)
-            nc.gpsimd.tensor_tensor(out=rstd[:], in0=var_eps[:], in1=minus_half[:], op=ALU.pow)
+            for bt in range(BATCH_TILES):
+                nc.scalar.activation(
+                    out=rstd[:, bt : bt + 1],
+                    in_=square_sums[:, bt, last : last + 1],
+                    func=ACT.Abs_reciprocal_sqrt,
+                    scale=1.0 / WIDTH,
+                    bias=root_bias[:, bt : bt + 1],
+                )
 
-            exps = []
+            c_of = []
             for j in range(GROUPS):
-                f_cols = slice(j * P, (j + 1) * P)
                 z_cols = [
-                    z_flips.tile([P, 2, BATCH], F32, name="z_cols%d" % pair, tag="z_cols")
+                    turns.tile([P, 2, BATCH], F32, name="z_cols%d" % pair, tag="turn")
                     for pair in range(VARIABLES // 2)
                 ]
                 for bt in range(BATCH_TILES):
-                    z = work.tile([P, VARIABLES, P], F32, bufs=4)
+                    z = work.tile([P, VARIABLES, P], F32)
                     nc.vector.tensor_scalar(
                         out=z[:],
-                        in0=r[bt][:].rearrange("p (v f) -> p v f", v=VARIABLES)[:, :, f_cols],
+                        in0=r[bt][:].rearrange("p (v f) -> p v f", v=VARIABLES)[:, :, j * P : (j + 1) * P],
                         scalar1=minus_mean[:, bt : bt + 1],
                         scalar2=rstd[:, bt : bt + 1],
                         op0=ALU.add,
@@ -324,55 +322,57 @@ def tile_variableselectionnetwork_pa_kernel(
                         scale=vector_col(GAIN, s),
                         bias=vector_col(SHIFT, s),
                     )
-                top2 = work.tile([P, 2, BATCH], F32, tag="pair")
-                nc.vector.tensor_max(out=top2[:], in0=c[:, 0:2, :], in1=c[:, 2:4, :])
-                top = work.tile([P, BATCH], F32)
-                nc.vector.tensor_max(out=top[:], in0=top2[:, 0, :], in1=top2[:, 1, :])
-                nc.vector.tensor_sub(
-                    out=c[:], in0=c[:], in1=top[:].unsqueeze(1).to_broadcast([P, VARIABLES, BATCH])
-                )
-                nc.scalar.activation(out=c[:], in_=c[:], func=ACT.Exp)
-                exps.append(c)
+                c_of.append(c)
 
-            inverses = []
+            e_rows_of = {}
+            for pair in ((0, 1), (2, 3)):
+                top2_of = {}
+                top_of = {}
+                for j in pair:
+                    top2_of[j] = work.tile([P, 2, BATCH], F32, name="top2")
+                    nc.vector.tensor_max(out=top2_of[j][:], in0=c_of[j][:, 0:2, :], in1=c_of[j][:, 2:4, :])
+                for j in pair:
+                    top_of[j] = work.tile([P, BATCH], F32, name="top")
+                    nc.vector.tensor_max(out=top_of[j][:], in0=top2_of[j][:, 0, :], in1=top2_of[j][:, 1, :])
+                for j in pair:
+                    nc.vector.tensor_sub(
+                        out=c_of[j][:],
+                        in0=c_of[j][:],
+                        in1=top_of[j][:].unsqueeze(1).to_broadcast([P, VARIABLES, BATCH]),
+                    )
+                    nc.scalar.activation(out=c_of[j][:], in_=c_of[j][:], func=ACT.Exp)
+                    for bt in range(BATCH_TILES):
+                        e_rows = turns.tile([P, VARIABLES, P], F32, tag="turn")
+                        for v in range(VARIABLES):
+                            nc.tensor.transpose(
+                                out=e_rows[:, v, :],
+                                in_=c_of[j][:, v, bt * P : (bt + 1) * P],
+                                identity=ident_f32[:],
+                            )
+                        e_rows_of[(j, bt)] = e_rows
+
+            inv_of = []
             for j in range(GROUPS):
-                e = exps[j]
-                sum2 = work.tile([P, 2, BATCH], F32, tag="pair")
-                nc.vector.tensor_add(out=sum2[:], in0=e[:, 0:2, :], in1=e[:, 2:4, :])
-                denom = per_group.tile([P, BATCH], F32)
-                nc.vector.tensor_add(out=denom[:], in0=sum2[:, 0, :], in1=sum2[:, 1, :])
-                inverses.append(denom)
-            for j in range(GROUPS):
-                inv = inverses[j]
+                inv = per_group.tile([P, BATCH_TILES, P], F32)
+                for bt in range(BATCH_TILES):
+                    nc.vector.tensor_reduce(
+                        out=inv[:, bt, :],
+                        in_=e_rows_of[(j, bt)][:].rearrange("p v f -> p f v"),
+                        axis=AXIS.X,
+                        op=ALU.add,
+                    )
                 nc.scalar.activation(out=inv[:], in_=inv[:], func=ACT.Abs_reciprocal_sqrt)
                 nc.scalar.activation(out=inv[:], in_=inv[:], func=ACT.Square)
+                inv_of.append(inv)
 
             for j in range(GROUPS):
-                f_cols = slice(j * P, (j + 1) * P)
-                e_rows = []
                 for bt in range(BATCH_TILES):
-                    rows = e_flips.tile([P, VARIABLES, P], F32, name="e_rows%d" % bt, tag="e_rows")
-                    for v in range(VARIABLES):
-                        nc.tensor.transpose(
-                            out=rows[:, v, :],
-                            in_=exps[j][:, v, bt * P : (bt + 1) * P],
-                            identity=ident_f32[:],
-                        )
-                    e_rows.append(rows)
-                inv_flip = inv_flips.tile([P, BATCH_TILES, P], F32)
-                for bt in range(BATCH_TILES):
-                    nc.tensor.transpose(
-                        out=inv_flip[:, bt, :],
-                        in_=inverses[j][:, bt * P : (bt + 1) * P],
-                        identity=ident_f32[:],
-                    )
-                inv_rows = work.tile([P, BATCH_TILES, P], F32)
-                nc.scalar.copy(out=inv_rows[:], in_=inv_flip[:])
-                for bt in range(BATCH_TILES):
-                    result = work.tile([P, VARIABLES, P], F32, bufs=4)
+                    result = work.tile([P, VARIABLES, P], F32)
                     nc.vector.tensor_mul(
                         out=result[:],
-                        in0=e_rows[bt][:],
-                        in1=inv_rows[:, bt, :].unsqueeze(1).to_broadcast([P, VARIABLES, P]),
+                        in0=e_rows_of[(j, bt)][:],
+                        in1=inv_of[j][:, bt, :].unsqueeze(1).to_broadcast([P, VARIABLES, P]),
                     )
-                    nc.sync.dma_start(out=out[bt * P : (bt + 1) * P, :, f_cols], in_=result[:])
+                    nc.sync.dma_start(
+                        out=out[bt * P : (bt + 1) * P, :, j * P : (j + 1) * P], in_=result[:]
+                    )

@@ -33,6 +33,9 @@ CB4 = 1
 CB5 = 2
 GAIN = 3
 SHIFT = 4
+SHARE_AFTER_CW1 = 17
+SHARE_AFTER_CW4 = 19
+SHARE_AFTER_CW5 = 12
 FIRST_LAYER_RANGES = ((0, HALF), (HALF, HALF))
 SECOND_LAYER_RANGES = ((0, HALF), (HALF, FEATURES), (HALF + FEATURES, FEATURES))
 
@@ -72,9 +75,9 @@ def tile_variableselectionnetwork_pa_kernel(
             return vector_cols[:, i * SLICES + s : i * SLICES + s + 1]
 
         with ExitStack() as stream:
-            raw_pool = stream.enter_context(tc.tile_pool(name="raw", bufs=5))
-            grouped_pool = stream.enter_context(tc.tile_pool(name="grouped", bufs=3))
-            codes_pool = stream.enter_context(tc.tile_pool(name="codes", bufs=3))
+            raw_pool = stream.enter_context(tc.tile_pool(name="raw", bufs=6))
+            grouped_pool = stream.enter_context(tc.tile_pool(name="grouped", bufs=5))
+            codes_pool = stream.enter_context(tc.tile_pool(name="codes", bufs=2))
             e1_pool = stream.enter_context(tc.tile_pool(name="e1", bufs=1))
             gate_pool = stream.enter_context(tc.tile_pool(name="gate", bufs=2))
             gated_pool = stream.enter_context(tc.tile_pool(name="gated", bufs=4))
@@ -82,49 +85,50 @@ def tile_variableselectionnetwork_pa_kernel(
             flips_bf = stream.enter_context(tc.psum_pool(name="flips_bf", bufs=2))
             flips_f32 = stream.enter_context(tc.psum_pool(name="flips_f32", bufs=2))
 
-            with tc.tile_pool(name="head", bufs=1) as head:
-                h_rows = []
-                for bt in range(BATCH_TILES):
-                    rows = head.tile([P, WIDTH], BF16, name="h_rows%d" % bt)
-                    nc.sync.dma_start(out=rows[:], in_=h[bt * P : (bt + 1) * P, :])
-                    h_rows.append(rows)
+            def quantise_h():
+                with tc.tile_pool(name="head", bufs=1) as head:
+                    h_rows = []
+                    for bt in range(BATCH_TILES):
+                        rows = head.tile([P, WIDTH], BF16, name="h_rows%d" % bt)
+                        nc.sync.dma_start(out=rows[:], in_=h[bt * P : (bt + 1) * P, :])
+                        h_rows.append(rows)
 
-                vector_rows = head.tile([P, P], BF16)
-                nc.vector.memset(vector_rows[:], 0.0)
-                for i, vec in enumerate((cb1, cb4, cb5, clng, clnb)):
-                    nc.scalar.dma_start(
-                        out=vector_rows[i * SLICES : (i + 1) * SLICES, :],
-                        in_=vec.rearrange("(s p) -> s p", p=P),
+                    vector_rows = head.tile([P, P], BF16)
+                    nc.vector.memset(vector_rows[:], 0.0)
+                    for i, vec in enumerate((cb1, cb4, cb5, clng, clnb)):
+                        nc.scalar.dma_start(
+                            out=vector_rows[i * SLICES : (i + 1) * SLICES, :],
+                            in_=vec.rearrange("(s p) -> s p", p=P),
+                        )
+
+                    h_grouped = head.tile([P, PASSES, BATCH, PACK], BF16, align_bytes=64)
+                    for g in range(PASSES):
+                        h_flip = flips_bf.tile([P, PACK, BATCH], BF16, tag="flip_bf")
+                        for t in range(PACK):
+                            k0 = g * K_PASS + t * P
+                            for bt in range(BATCH_TILES):
+                                nc.tensor.transpose(
+                                    out=h_flip[:, t, bt * P : (bt + 1) * P],
+                                    in_=h_rows[bt][:, k0 : k0 + P],
+                                    identity=ident_bf[:],
+                                )
+                        copy_out = nc.vector.tensor_copy if g % 2 == 0 else nc.scalar.copy
+                        copy_out(out=h_grouped[:, g, :, :], in_=h_flip[:].rearrange("p t b -> p b t"))
+                    nc.vector.quantize_mx(
+                        out=h_codes[:].rearrange("p g b -> p (g b)").bitcast(FP8X4),
+                        scales=h_scales[:].rearrange("p g b -> p (g b)"),
+                        in_=h_grouped[:].rearrange("p g b t -> p (g b t)"),
                     )
 
-                h_grouped = head.tile([P, PASSES, BATCH, PACK], BF16, align_bytes=64)
-                for g in range(PASSES):
-                    h_flip = flips_bf.tile([P, PACK, BATCH], BF16, tag="flip_bf")
-                    for t in range(PACK):
-                        k0 = g * K_PASS + t * P
-                        for bt in range(BATCH_TILES):
-                            nc.tensor.transpose(
-                                out=h_flip[:, t, bt * P : (bt + 1) * P],
-                                in_=h_rows[bt][:, k0 : k0 + P],
-                                identity=ident_bf[:],
-                            )
-                    copy_out = nc.vector.tensor_copy if g % 2 == 0 else nc.scalar.copy
-                    copy_out(out=h_grouped[:, g, :, :], in_=h_flip[:].rearrange("p t b -> p b t"))
-                nc.vector.quantize_mx(
-                    out=h_codes[:].rearrange("p g b -> p (g b)").bitcast(FP8X4),
-                    scales=h_scales[:].rearrange("p g b -> p (g b)"),
-                    in_=h_grouped[:].rearrange("p g b t -> p (g b t)"),
-                )
+                    vector_flip = flips_bf.tile([P, P], BF16, tag="flip_bf")
+                    nc.tensor.transpose(out=vector_flip[:], in_=vector_rows[:], identity=ident_bf[:])
+                    nc.vector.tensor_copy(out=vector_cols[:], in_=vector_flip[:])
 
-                vector_flip = flips_bf.tile([P, P], BF16, tag="flip_bf")
-                nc.tensor.transpose(out=vector_flip[:], in_=vector_rows[:], identity=ident_bf[:])
-                nc.vector.tensor_copy(out=vector_cols[:], in_=vector_flip[:])
-
-            def quantise_columns(w, first, width):
+            def quantise_columns(w, first, width, vector_share):
                 codes = codes_pool.tile([P, PASSES, width], U32, align_bytes=64, tag="codes")
                 scales = codes_pool.tile([P, PASSES, width], U8, align_bytes=64, tag="scales")
                 w_passes = w.rearrange("(g t p) n -> g p t n", t=PACK, p=P)
-                split = width // 2
+                split = width * vector_share // 32
                 for g in range(PASSES):
                     raw = raw_pool.tile([P, PACK, width], BF16, tag="raw")
                     nc.sync.dma_start(out=raw[:], in_=w_passes[g][:, :, first : first + width])
@@ -140,97 +144,101 @@ def tile_variableselectionnetwork_pa_kernel(
                     )
                 return codes, scales
 
-            def product_slice(codes, scales, j, act_codes, act_scales):
-                acc = sums.tile([P, BATCH], F32)
-                feats = slice(j * P, (j + 1) * P)
+            def products(codes, scales, j0, act_codes, act_scales):
+                accs = [sums.tile([P, BATCH], F32, name="acc%d" % i, tag="acc") for i in range(PACK)]
                 for g in range(PASSES):
-                    nc.tensor.matmul_mx(
-                        out=acc[:],
-                        lhsT=codes[:, g, feats].bitcast(FP8X4),
-                        lhsT_scale=scales[:, g, feats],
-                        rhs=act_codes[:, g, :].bitcast(FP8X4),
-                        rhs_scale=act_scales[:, g, :],
-                        start=(g == 0),
-                        stop=(g == PASSES - 1),
-                    )
-                return acc
+                    for i in range(PACK):
+                        feats = slice((j0 + i) * P, (j0 + i + 1) * P)
+                        nc.tensor.matmul_mx(
+                            out=accs[i][:],
+                            lhsT=codes[:, g, feats].bitcast(FP8X4),
+                            lhsT_scale=scales[:, g, feats],
+                            rhs=act_codes[:, g, :].bitcast(FP8X4),
+                            rhs_scale=act_scales[:, g, :],
+                            start=(g == 0),
+                            stop=(g == PASSES - 1),
+                        )
+                return accs
 
             e1_bf = e1_pool.tile([P, PASSES, PACK, BATCH], BF16)
             e1_grouped = e1_pool.tile([P, PASSES, BATCH, PACK], BF16, align_bytes=64)
             for first, width in FIRST_LAYER_RANGES:
-                codes, scales = quantise_columns(cW1, first, width)
-                for j in range(width // P):
-                    s = first // P + j
-                    g2, t2 = divmod(s, PACK)
-                    acc = product_slice(codes, scales, j, h_codes, h_scales)
-                    nc.scalar.activation(
-                        out=e1_bf[:, g2, t2, :],
-                        in_=acc[:],
-                        func=ACT.Identity,
-                        bias=vector_col(CB1, s),
-                        scale=1.0,
-                    )
-                    if t2 == PACK - 1:
-                        dst, src = word_order(e1_grouped[:, g2, :, :], e1_bf[:, g2, :, :])
-                        nc.vector.tensor_copy(out=dst, in_=src)
-                        nc.vector.quantize_mx(
-                            out=e1_codes[:, g2, :].bitcast(FP8X4),
-                            scales=e1_scales[:, g2, :],
-                            in_=e1_grouped[:, g2, :, :].rearrange("p b t -> p (b t)"),
+                codes, scales = quantise_columns(cW1, first, width, SHARE_AFTER_CW1)
+                if first == 0:
+                    quantise_h()
+                for j0 in range(0, width // P, PACK):
+                    g2 = (first // P + j0) // PACK
+                    accs = products(codes, scales, j0, h_codes, h_scales)
+                    for t2 in range(PACK):
+                        nc.scalar.activation(
+                            out=e1_bf[:, g2, t2, :],
+                            in_=accs[t2][:],
+                            func=ACT.Identity,
+                            bias=vector_col(CB1, g2 * PACK + t2),
+                            scale=1.0,
                         )
+                    dst, src = word_order(e1_grouped[:, g2, :, :], e1_bf[:, g2, :, :])
+                    nc.vector.tensor_copy(out=dst, in_=src)
+                    nc.vector.quantize_mx(
+                        out=e1_codes[:, g2, :].bitcast(FP8X4),
+                        scales=e1_scales[:, g2, :],
+                        in_=e1_grouped[:, g2, :, :].rearrange("p b t -> p (b t)"),
+                    )
 
             for bt in range(BATCH_TILES):
                 nc.sync.dma_start(out=x_sb[bt][:], in_=x_rows[bt * P : (bt + 1) * P, :])
 
             for first, width in SECOND_LAYER_RANGES:
-                codes, scales = quantise_columns(cW4, first, width)
+                codes, scales = quantise_columns(
+                    cW4, first, width, SHARE_AFTER_CW1 if first == 0 else SHARE_AFTER_CW5
+                )
                 gate = gate_pool.tile([P, HALF // P, BATCH], F32)
-                for j in range(width // P):
-                    s = first // P + j
-                    acc = product_slice(codes, scales, j, e1_codes, e1_scales)
-                    nc.scalar.activation(
-                        out=gate[:, j, :],
-                        in_=acc[:],
-                        func=ACT.Sigmoid,
-                        bias=vector_col(CB4, s),
-                        scale=1.0,
-                    )
+                for j0 in range(0, width // P, PACK):
+                    accs = products(codes, scales, j0, e1_codes, e1_scales)
+                    for i in range(PACK):
+                        nc.scalar.activation(
+                            out=gate[:, j0 + i, :],
+                            in_=accs[i][:],
+                            func=ACT.Sigmoid,
+                            bias=vector_col(CB4, first // P + j0 + i),
+                            scale=1.0,
+                        )
                 if first + width == WIDTH:
                     warm = gate_pool.tile([P, 1], F32)
                     nc.scalar.activation(
                         out=warm[:], in_=ident_f32[:, 0:1], func=ACT.Abs_reciprocal_sqrt, bias=1.0
                     )
 
-                codes, scales = quantise_columns(cW5, first, width)
+                codes, scales = quantise_columns(cW5, first, width, SHARE_AFTER_CW4)
                 for v_local in range(width // FEATURES):
                     v = first // FEATURES + v_local
-                    gated = []
+                    j0 = v_local * SLICES_PER_VARIABLE
+                    accs = products(codes, scales, j0, e1_codes, e1_scales)
+                    g_rows = [
+                        flips_f32.tile([P, FEATURES], F32, name="g_rows%d" % bt, tag="g_rows")
+                        for bt in range(BATCH_TILES)
+                    ]
                     for i in range(SLICES_PER_VARIABLE):
-                        j = v_local * SLICES_PER_VARIABLE + i
-                        s = first // P + j
-                        acc = product_slice(codes, scales, j, e1_codes, e1_scales)
                         g_slice = gated_pool.tile([P, BATCH], F32)
                         nc.vector.scalar_tensor_tensor(
                             out=g_slice[:],
-                            in0=acc[:],
-                            scalar=vector_col(CB5, s),
-                            in1=gate[:, j, :],
+                            in0=accs[i][:],
+                            scalar=vector_col(CB5, first // P + j0 + i),
+                            in1=gate[:, j0 + i, :],
                             op0=ALU.add,
                             op1=ALU.mult,
                         )
-                        gated.append(g_slice)
-                    v_cols = slice(v * FEATURES, (v + 1) * FEATURES)
-                    for bt in range(BATCH_TILES):
-                        g_rows = flips_f32.tile([P, FEATURES], F32)
-                        for i in range(SLICES_PER_VARIABLE):
+                        for bt in range(BATCH_TILES):
                             nc.tensor.transpose(
-                                out=g_rows[:, i * P : (i + 1) * P],
-                                in_=gated[i][:, bt * P : (bt + 1) * P],
+                                out=g_rows[bt][:, i * P : (i + 1) * P],
+                                in_=g_slice[:, bt * P : (bt + 1) * P],
                                 identity=ident_f32[:],
                             )
+                    v_cols = slice(v * FEATURES, (v + 1) * FEATURES)
+                    for bt in range(BATCH_TILES):
                         nc.vector.scalar_tensor_tensor(
                             out=r[bt][:, v_cols],
-                            in0=g_rows[:],
+                            in0=g_rows[bt][:],
                             scalar=1.0,
                             in1=x_sb[bt][:, v_cols],
                             op0=ALU.mult,

@@ -33,9 +33,9 @@ CB4 = 1
 CB5 = 2
 GAIN = 3
 SHIFT = 4
-SHARE_AFTER_CW1 = 17
-SHARE_AFTER_CW4 = 19
-SHARE_AFTER_CW5 = 12
+SHARE_AFTER_CW1 = 16
+SHARE_AFTER_CW4 = 18
+SHARE_AFTER_CW5 = 11
 FIRST_LAYER_RANGES = ((0, HALF), (HALF, HALF))
 SECOND_LAYER_RANGES = ((0, HALF), (HALF, FEATURES), (HALF + FEATURES, FEATURES))
 
@@ -301,8 +301,8 @@ def tile_variableselectionnetwork_pa_kernel(
             c_of = []
             for j in range(GROUPS):
                 z_cols = [
-                    turns.tile([P, 2, BATCH], F32, name="z_cols%d" % pair, tag="turn")
-                    for pair in range(VARIABLES // 2)
+                    turns.tile([P, 2, BATCH], F32, name="z_cols%d" % bank, tag="turn")
+                    for bank in range(VARIABLES // 2)
                 ]
                 for bt in range(BATCH_TILES):
                     z = work.tile([P, VARIABLES, P], F32)
@@ -333,7 +333,8 @@ def tile_variableselectionnetwork_pa_kernel(
                 c_of.append(c)
 
             e_rows_of = {}
-            for pair in ((0, 1), (2, 3)):
+            for j0 in range(0, GROUPS, 2):
+                pair = (j0, j0 + 1)
                 top2_of = {}
                 top_of = {}
                 for j in pair:

from contextlib import ExitStack

import concourse.mybir as mybir
from concourse.masks import make_identity

FLOPS = 2 * 256 * 2048 * 2048 * 3

BF16 = mybir.dt.bfloat16
F32 = mybir.dt.float32
U32 = mybir.dt.uint32
U8 = mybir.dt.uint8
FP8X4 = mybir.dt.float8_e4m3fn_x4
ALU = mybir.AluOpType
ACT = mybir.ActivationFunctionType
AXIS = mybir.AxisListType

P = 128
PACK = 4
K_PASS = P * PACK
BATCH = 256
BATCH_TILES = BATCH // P
WIDTH = 2048
PASSES = WIDTH // K_PASS
VARIABLES = 4
FEATURES = WIDTH // VARIABLES
HALF = WIDTH // 2
SLICES_PER_VARIABLE = FEATURES // P
SLICES = WIDTH // P
GROUPS = SLICES_PER_VARIABLE
EPS = 1e-5
CB1 = 0
CB4 = 1
CB5 = 2
GAIN = 3
SHIFT = 4
SHARE_AFTER_CW1 = 16
SHARE_AFTER_CW4 = 18
SHARE_AFTER_CW5 = 11
FIRST_LAYER_RANGES = ((0, HALF), (HALF, HALF))
SECOND_LAYER_RANGES = ((0, HALF), (HALF, FEATURES), (HALF + FEATURES, FEATURES))


def word_order(dst, src):
    return (
        dst.rearrange("p (c i) t -> p c t i", i=4),
        src.rearrange("p t (c i) -> p c t i", i=4),
    )


def tile_variableselectionnetwork_pa_kernel(
    tc, h, x, cW1, cb1, cW4, cb4, cW5, cb5, clng, clnb, out
):
    nc = tc.nc
    x_rows = x.rearrange("b v f -> b (v f)")

    with tc.tile_pool(name="keep", bufs=1) as keep:
        ident_bf = keep.tile([P, P], BF16)
        make_identity(nc, ident_bf[:])
        ident_f32 = keep.tile([P, P], F32)
        make_identity(nc, ident_f32[:])

        h_codes = keep.tile([P, PASSES, BATCH], U32, align_bytes=64)
        h_scales = keep.tile([P, PASSES, BATCH], U8, align_bytes=64)
        e1_codes = keep.tile([P, PASSES, BATCH], U32, align_bytes=64)
        e1_scales = keep.tile([P, PASSES, BATCH], U8, align_bytes=64)
        x_sb = [keep.tile([P, WIDTH], BF16, name="x_sb%d" % bt) for bt in range(BATCH_TILES)]
        r = [keep.tile([P, WIDTH], F32, name="r%d" % bt) for bt in range(BATCH_TILES)]
        r_sums = keep.tile([P, BATCH_TILES, VARIABLES], F32)
        minus_shift = keep.tile([P, BATCH_TILES], F32)
        square_sums = keep.tile([P, BATCH_TILES, VARIABLES], F32)

        vector_cols = keep.tile([P, P], F32)

        def vector_col(i, s):
            return vector_cols[:, i * SLICES + s : i * SLICES + s + 1]

        with ExitStack() as stream:
            raw_pool = stream.enter_context(tc.tile_pool(name="raw", bufs=6))
            grouped_pool = stream.enter_context(tc.tile_pool(name="grouped", bufs=5))
            codes_pool = stream.enter_context(tc.tile_pool(name="codes", bufs=2))
            e1_pool = stream.enter_context(tc.tile_pool(name="e1", bufs=1))
            gate_pool = stream.enter_context(tc.tile_pool(name="gate", bufs=2))
            gated_pool = stream.enter_context(tc.tile_pool(name="gated", bufs=4))
            sums = stream.enter_context(tc.psum_pool(name="sums", bufs=4))
            flips_bf = stream.enter_context(tc.psum_pool(name="flips_bf", bufs=2))
            flips_f32 = stream.enter_context(tc.psum_pool(name="flips_f32", bufs=2))

            def quantise_h():
                with tc.tile_pool(name="head", bufs=1) as head:
                    h_rows = []
                    for bt in range(BATCH_TILES):
                        rows = head.tile([P, WIDTH], BF16, name="h_rows%d" % bt)
                        nc.sync.dma_start(out=rows[:], in_=h[bt * P : (bt + 1) * P, :])
                        h_rows.append(rows)

                    vector_rows = head.tile([P, P], BF16)
                    nc.vector.memset(vector_rows[:], 0.0)
                    for i, vec in enumerate((cb1, cb4, cb5, clng, clnb)):
                        nc.scalar.dma_start(
                            out=vector_rows[i * SLICES : (i + 1) * SLICES, :],
                            in_=vec.rearrange("(s p) -> s p", p=P),
                        )

                    h_grouped = head.tile([P, PASSES, BATCH, PACK], BF16, align_bytes=64)
                    for g in range(PASSES):
                        h_flip = flips_bf.tile([P, PACK, BATCH], BF16, tag="flip_bf")
                        for t in range(PACK):
                            k0 = g * K_PASS + t * P
                            for bt in range(BATCH_TILES):
                                nc.tensor.transpose(
                                    out=h_flip[:, t, bt * P : (bt + 1) * P],
                                    in_=h_rows[bt][:, k0 : k0 + P],
                                    identity=ident_bf[:],
                                )
                        copy_out = nc.vector.tensor_copy if g % 2 == 0 else nc.scalar.copy
                        copy_out(out=h_grouped[:, g, :, :], in_=h_flip[:].rearrange("p t b -> p b t"))
                    nc.vector.quantize_mx(
                        out=h_codes[:].rearrange("p g b -> p (g b)").bitcast(FP8X4),
                        scales=h_scales[:].rearrange("p g b -> p (g b)"),
                        in_=h_grouped[:].rearrange("p g b t -> p (g b t)"),
                    )

                    vector_flip = flips_bf.tile([P, P], BF16, tag="flip_bf")
                    nc.tensor.transpose(out=vector_flip[:], in_=vector_rows[:], identity=ident_bf[:])
                    nc.vector.tensor_copy(out=vector_cols[:], in_=vector_flip[:])

            def quantise_columns(w, first, width, vector_share):
                codes = codes_pool.tile([P, PASSES, width], U32, align_bytes=64, tag="codes")
                scales = codes_pool.tile([P, PASSES, width], U8, align_bytes=64, tag="scales")
                w_passes = w.rearrange("(g t p) n -> g p t n", t=PACK, p=P)
                split = width * vector_share // 32
                for g in range(PASSES):
                    raw = raw_pool.tile([P, PACK, width], BF16, tag="raw")
                    nc.sync.dma_start(out=raw[:], in_=w_passes[g][:, :, first : first + width])
                    grouped = grouped_pool.tile([P, width, PACK], BF16, align_bytes=64, tag="grouped")
                    dst, src = word_order(grouped[:, :split, :], raw[:, :, :split])
                    nc.vector.tensor_copy(out=dst, in_=src)
                    dst, src = word_order(grouped[:, split:, :], raw[:, :, split:])
                    nc.scalar.copy(out=dst, in_=src)
                    nc.vector.quantize_mx(
                        out=codes[:, g, :].bitcast(FP8X4),
                        scales=scales[:, g, :],
                        in_=grouped[:].rearrange("p c t -> p (c t)"),
                    )
                return codes, scales

            def products(codes, scales, j0, act_codes, act_scales):
                accs = [sums.tile([P, BATCH], F32, name="acc%d" % i, tag="acc") for i in range(PACK)]
                for g in range(PASSES):
                    for i in range(PACK):
                        feats = slice((j0 + i) * P, (j0 + i + 1) * P)
                        nc.tensor.matmul_mx(
                            out=accs[i][:],
                            lhsT=codes[:, g, feats].bitcast(FP8X4),
                            lhsT_scale=scales[:, g, feats],
                            rhs=act_codes[:, g, :].bitcast(FP8X4),
                            rhs_scale=act_scales[:, g, :],
                            start=(g == 0),
                            stop=(g == PASSES - 1),
                        )
                return accs

            e1_bf = e1_pool.tile([P, PASSES, PACK, BATCH], BF16)
            e1_grouped = e1_pool.tile([P, PASSES, BATCH, PACK], BF16, align_bytes=64)
            for first, width in FIRST_LAYER_RANGES:
                codes, scales = quantise_columns(cW1, first, width, SHARE_AFTER_CW1)
                if first == 0:
                    quantise_h()
                for j0 in range(0, width // P, PACK):
                    g2 = (first // P + j0) // PACK
                    accs = products(codes, scales, j0, h_codes, h_scales)
                    for t2 in range(PACK):
                        nc.scalar.activation(
                            out=e1_bf[:, g2, t2, :],
                            in_=accs[t2][:],
                            func=ACT.Identity,
                            bias=vector_col(CB1, g2 * PACK + t2),
                            scale=1.0,
                        )
                    dst, src = word_order(e1_grouped[:, g2, :, :], e1_bf[:, g2, :, :])
                    nc.vector.tensor_copy(out=dst, in_=src)
                    nc.vector.quantize_mx(
                        out=e1_codes[:, g2, :].bitcast(FP8X4),
                        scales=e1_scales[:, g2, :],
                        in_=e1_grouped[:, g2, :, :].rearrange("p b t -> p (b t)"),
                    )

            for bt in range(BATCH_TILES):
                nc.sync.dma_start(out=x_sb[bt][:], in_=x_rows[bt * P : (bt + 1) * P, :])

            for first, width in SECOND_LAYER_RANGES:
                codes, scales = quantise_columns(
                    cW4, first, width, SHARE_AFTER_CW1 if first == 0 else SHARE_AFTER_CW5
                )
                gate = gate_pool.tile([P, HALF // P, BATCH], F32)
                for j0 in range(0, width // P, PACK):
                    accs = products(codes, scales, j0, e1_codes, e1_scales)
                    for i in range(PACK):
                        nc.scalar.activation(
                            out=gate[:, j0 + i, :],
                            in_=accs[i][:],
                            func=ACT.Sigmoid,
                            bias=vector_col(CB4, first // P + j0 + i),
                            scale=1.0,
                        )
                if first + width == WIDTH:
                    warm = gate_pool.tile([P, 1], F32)
                    nc.scalar.activation(
                        out=warm[:], in_=ident_f32[:, 0:1], func=ACT.Abs_reciprocal_sqrt, bias=1.0
                    )

                codes, scales = quantise_columns(cW5, first, width, SHARE_AFTER_CW4)
                for v_local in range(width // FEATURES):
                    v = first // FEATURES + v_local
                    j0 = v_local * SLICES_PER_VARIABLE
                    accs = products(codes, scales, j0, e1_codes, e1_scales)
                    g_rows = [
                        flips_f32.tile([P, FEATURES], F32, name="g_rows%d" % bt, tag="g_rows")
                        for bt in range(BATCH_TILES)
                    ]
                    for i in range(SLICES_PER_VARIABLE):
                        g_slice = gated_pool.tile([P, BATCH], F32)
                        nc.vector.scalar_tensor_tensor(
                            out=g_slice[:],
                            in0=accs[i][:],
                            scalar=vector_col(CB5, first // P + j0 + i),
                            in1=gate[:, j0 + i, :],
                            op0=ALU.add,
                            op1=ALU.mult,
                        )
                        for bt in range(BATCH_TILES):
                            nc.tensor.transpose(
                                out=g_rows[bt][:, i * P : (i + 1) * P],
                                in_=g_slice[:, bt * P : (bt + 1) * P],
                                identity=ident_f32[:],
                            )
                    v_cols = slice(v * FEATURES, (v + 1) * FEATURES)
                    for bt in range(BATCH_TILES):
                        nc.vector.scalar_tensor_tensor(
                            out=r[bt][:, v_cols],
                            in0=g_rows[bt][:],
                            scalar=1.0,
                            in1=x_sb[bt][:, v_cols],
                            op0=ALU.mult,
                            op1=ALU.add,
                            accum_out=r_sums[:, bt, v : v + 1],
                        )
                        if v == 0:
                            nc.vector.tensor_scalar_mul(
                                out=minus_shift[:, bt : bt + 1],
                                in0=r_sums[:, bt, 0:1],
                                scalar1=-1.0 / FEATURES,
                            )
                        squares = gated_pool.tile([P, FEATURES], BF16)
                        nc.scalar.activation(
                            out=squares[:],
                            in_=r[bt][:, v_cols],
                            func=ACT.Square,
                            bias=minus_shift[:, bt : bt + 1],
                            scale=1.0,
                            accum_out=square_sums[:, bt, v : v + 1],
                        )

        with ExitStack() as finish:
            finish.enter_context(tc.manual_schedule())
            small = finish.enter_context(tc.tile_pool(name="small", bufs=1))
            work = finish.enter_context(tc.tile_pool(name="work", bufs=4))
            per_group = finish.enter_context(tc.tile_pool(name="per_group", bufs=GROUPS))
            turns = finish.enter_context(tc.psum_pool(name="turns", bufs=8))

            shape = [P, BATCH_TILES]
            last = VARIABLES - 1
            total = small.tile(shape, F32)
            nc.vector.tensor_reduce(out=total[:], in_=r_sums[:], axis=AXIS.X, op=ALU.add)
            minus_mean = small.tile(shape, F32)
            nc.vector.tensor_scalar_mul(out=minus_mean[:], in0=total[:], scalar1=-1.0 / WIDTH)
            offset = small.tile(shape, F32)
            nc.vector.tensor_sub(out=offset[:], in0=minus_mean[:], in1=minus_shift[:])
            minus_offset2 = small.tile(shape, F32)
            nc.vector.scalar_tensor_tensor(
                out=minus_offset2[:], in0=offset[:], scalar=-1.0, in1=offset[:], op0=ALU.mult, op1=ALU.mult
            )
            early = small.tile(shape, F32)
            nc.vector.tensor_reduce(out=early[:], in_=square_sums[:, :, :last], axis=AXIS.X, op=ALU.add)
            early_eps = small.tile(shape, F32)
            nc.vector.tensor_scalar(
                out=early_eps[:], in0=early[:], scalar1=1.0 / WIDTH, scalar2=EPS, op0=ALU.mult, op1=ALU.add
            )
            root_bias = small.tile(shape, F32)
            nc.vector.tensor_add(out=root_bias[:], in0=early_eps[:], in1=minus_offset2[:])
            rstd = small.tile(shape, F32)
            for bt in range(BATCH_TILES):
                nc.scalar.activation(
                    out=rstd[:, bt : bt + 1],
                    in_=square_sums[:, bt, last : last + 1],
                    func=ACT.Abs_reciprocal_sqrt,
                    scale=1.0 / WIDTH,
                    bias=root_bias[:, bt : bt + 1],
                )

            c_of = []
            for j in range(GROUPS):
                z_cols = [
                    turns.tile([P, 2, BATCH], F32, name="z_cols%d" % bank, tag="turn")
                    for bank in range(VARIABLES // 2)
                ]
                for bt in range(BATCH_TILES):
                    z = work.tile([P, VARIABLES, P], F32)
                    nc.vector.tensor_scalar(
                        out=z[:],
                        in0=r[bt][:].rearrange("p (v f) -> p v f", v=VARIABLES)[:, :, j * P : (j + 1) * P],
                        scalar1=minus_mean[:, bt : bt + 1],
                        scalar2=rstd[:, bt : bt + 1],
                        op0=ALU.add,
                        op1=ALU.mult,
                    )
                    for v in range(VARIABLES):
                        nc.tensor.transpose(
                            out=z_cols[v // 2][:, v % 2, bt * P : (bt + 1) * P],
                            in_=z[:, v, :],
                            identity=ident_f32[:],
                        )
                c = per_group.tile([P, VARIABLES, BATCH], F32)
                for v in range(VARIABLES):
                    s = v * SLICES_PER_VARIABLE + j
                    nc.scalar.activation(
                        out=c[:, v, :],
                        in_=z_cols[v // 2][:, v % 2, :],
                        func=ACT.Identity,
                        scale=vector_col(GAIN, s),
                        bias=vector_col(SHIFT, s),
                    )
                c_of.append(c)

            e_rows_of = {}
            for j0 in range(0, GROUPS, 2):
                pair = (j0, j0 + 1)
                top2_of = {}
                top_of = {}
                for j in pair:
                    top2_of[j] = work.tile([P, 2, BATCH], F32, name="top2")
                    nc.vector.tensor_max(out=top2_of[j][:], in0=c_of[j][:, 0:2, :], in1=c_of[j][:, 2:4, :])
                for j in pair:
                    top_of[j] = work.tile([P, BATCH], F32, name="top")
                    nc.vector.tensor_max(out=top_of[j][:], in0=top2_of[j][:, 0, :], in1=top2_of[j][:, 1, :])
                for j in pair:
                    nc.vector.tensor_sub(
                        out=c_of[j][:],
                        in0=c_of[j][:],
                        in1=top_of[j][:].unsqueeze(1).to_broadcast([P, VARIABLES, BATCH]),
                    )
                    nc.scalar.activation(out=c_of[j][:], in_=c_of[j][:], func=ACT.Exp)
                    for bt in range(BATCH_TILES):
                        e_rows = turns.tile([P, VARIABLES, P], F32, tag="turn")
                        for v in range(VARIABLES):
                            nc.tensor.transpose(
                                out=e_rows[:, v, :],
                                in_=c_of[j][:, v, bt * P : (bt + 1) * P],
                                identity=ident_f32[:],
                            )
                        e_rows_of[(j, bt)] = e_rows

            inv_of = []
            for j in range(GROUPS):
                inv = per_group.tile([P, BATCH_TILES, P], F32)
                for bt in range(BATCH_TILES):
                    nc.vector.tensor_reduce(
                        out=inv[:, bt, :],
                        in_=e_rows_of[(j, bt)][:].rearrange("p v f -> p f v"),
                        axis=AXIS.X,
                        op=ALU.add,
                    )
                nc.scalar.activation(out=inv[:], in_=inv[:], func=ACT.Abs_reciprocal_sqrt)
                nc.scalar.activation(out=inv[:], in_=inv[:], func=ACT.Square)
                inv_of.append(inv)

            for j in range(GROUPS):
                for bt in range(BATCH_TILES):
                    result = work.tile([P, VARIABLES, P], F32)
                    nc.vector.tensor_mul(
                        out=result[:],
                        in0=e_rows_of[(j, bt)][:],
                        in1=inv_of[j][:, bt, :].unsqueeze(1).to_broadcast([P, VARIABLES, P]),
                    )
                    nc.sync.dma_start(
                        out=out[bt * P : (bt + 1) * P, :, j * P : (j + 1) * P], in_=result[:]
                    )
